import numpy as np
import ml_dtypes


def mxq(x, axis, fmt="e4m3"):
    dtype, down = {"e4m3": (ml_dtypes.float8_e4m3fn, 7), "e5m2": (ml_dtypes.float8_e5m2, 14)}[fmt]
    v = np.moveaxis(np.asarray(x, np.float32).astype(ml_dtypes.bfloat16).astype(np.float64), axis, -1)
    blocks = v.reshape(v.shape[:-1] + (-1, 32))
    amax = np.abs(blocks).max(-1, keepdims=True)
    byte = np.maximum(np.where(amax > 0, np.frexp(amax)[1] - 1 + 127, 0) - down, 1)
    scale = np.exp2(byte - 127.0)
    codes = (blocks / scale).astype(np.float32).astype(dtype).astype(np.float64)
    return np.moveaxis((codes * scale).reshape(v.shape), -1, axis)


WIDE = False


def mx_kscale(k):
    if not WIDE:
        return np.ones(k)
    levels = np.array([10, -10, 5, -5, 0])
    a = np.random.permutation(np.resize(levels, k // 512 * 4)).reshape(k // 512, 4)
    idx = np.arange(k)
    return np.exp2(a[idx // 512, idx % 128 // 32])


BF16 = ml_dtypes.bfloat16


def bf(x):
    return np.asarray(x, np.float32).astype(BF16)


def f64(x):
    return np.asarray(x).astype(np.float64)


N, C, O, TH, TW = 2, 1024, 512, 32, 64
BN_EPS = 1e-5
IMG_SIZES = [(max(TH >> (l + 1), 1), max(TW >> (l + 1), 1)) for l in range(5)]


def setup_inputs():
    s = mx_kscale(C)
    sc = s[None, :, None, None]
    inp = {}
    for l, (h, w) in enumerate(IMG_SIZES):
        inp[f'img_feat{l}'] = bf(np.random.standard_normal((N, C, h, w)) * 0.5 * sc)
    inp['pts_feat0'] = bf(np.random.standard_normal((N, C, TH, TW)) * sc)
    inp['img_w'] = bf(np.random.standard_normal((O, C)) / np.sqrt(C) / s[None, :])
    inp['img_b'] = bf(np.random.standard_normal(O) * 0.1)
    inp['img_gamma'] = bf(1.0 + 0.1 * np.random.standard_normal(O))
    inp['img_beta'] = bf(np.random.standard_normal(O) * 0.1)
    inp['img_mean'] = bf(np.random.standard_normal(O) * 0.1)
    inp['img_var'] = bf(np.random.uniform(0.5, 1.5, O))
    inp['pts_w'] = bf(np.random.standard_normal((O, C)) / np.sqrt(C) / s[None, :])
    inp['pts_b'] = bf(np.random.standard_normal(O) * 0.1)
    inp['pts_gamma'] = bf(1.0 + 0.1 * np.random.standard_normal(O))
    inp['pts_beta'] = bf(np.random.standard_normal(O) * 0.1)
    inp['pts_mean'] = bf(np.random.standard_normal(O) * 0.1)
    inp['pts_var'] = bf(np.random.uniform(0.5, 1.5, O))
    return inp


def _obtain_mlvl(feats, th, tw):
    n = feats[0].shape[0]
    outs = []
    for i in range(n):
        acc = None
        for lvl, f in enumerate(feats):
            x = f[i]
            if lvl > 0:
                s = i + 1
                x = np.repeat(np.repeat(x, s, axis=1), s, axis=2)
            dh = th - x.shape[1]
            dw = tw - x.shape[2]
            x = np.pad(x, ((0, 0), (dh // 2, dh - dh // 2), (dw // 2, dw - dw // 2)), mode='edge')
            acc = x if acc is None else acc + x
        outs.append(acc)
    return np.stack(outs, 0)


def _conv_bn_relu(x, w, b, gamma, beta, mean, var):
    n, c, h, wd = x.shape
    y = (mxq(w, 1, 'e4m3') @ mxq(x, 1, 'e4m3').reshape(n, c, h * wd)).reshape(n, -1, h, wd) + b[None, :, None, None]
    scale = gamma / np.sqrt(var + BN_EPS)
    y = (y - mean[None, :, None, None]) * scale[None, :, None, None] + beta[None, :, None, None]
    return np.maximum(y, 0.0)


def reference(img_feat0, img_feat1, img_feat2, img_feat3, img_feat4, pts_feat0,
              img_w, img_b, img_gamma, img_beta, img_mean, img_var,
              pts_w, pts_b, pts_gamma, pts_beta, pts_mean, pts_var):
    th, tw = pts_feat0.shape[2], pts_feat0.shape[3]
    pts_m = _obtain_mlvl([f64(pts_feat0)], th, tw)
    pts_pre = _conv_bn_relu(pts_m, f64(pts_w), f64(pts_b), f64(pts_gamma), f64(pts_beta), f64(pts_mean), f64(pts_var))
    img_m = _obtain_mlvl([f64(img_feat0), f64(img_feat1), f64(img_feat2), f64(img_feat3), f64(img_feat4)], th, tw)
    img_pre = _conv_bn_relu(img_m, f64(img_w), f64(img_b), f64(img_gamma), f64(img_beta), f64(img_mean), f64(img_var))
    return np.concatenate((img_pre, pts_pre), axis=1)

@@ -1,0 +1,295 @@
+from contextlib import ExitStack
+
+import concourse.masks as masks
+import concourse.mybir as mybir
+
+FP8X4 = mybir.dt.float8_e4m3fn_x4
+BF16 = mybir.dt.bfloat16
+F32 = mybir.dt.float32
+U32 = mybir.dt.uint32
+U8 = mybir.dt.uint8
+ACT = mybir.ActivationFunctionType
+ALU = mybir.AluOpType
+
+P = 128
+NS = 2
+G = 2
+J = 4
+MT = 4
+HW = 2048
+NQ = 4
+CH, CW = 16, 32
+BN_EPS = 1e-5
+
+FLOPS = 2 * 2 * NS * 512 * 1024 * HW
+
+SCALAR_UNITS = ((0, 0, 0), (0, 0, 1), (0, 0, 2), (0, 0, 3), (1, 0, 0), (1, 0, 1))
+
+
+def spans(inner):
+    off = inner // 2
+    return ((0, off, 0, 1), (off, off + inner, 0, inner), (off + inner, 2 * inner, inner - 1, inner))
+
+
+def tile_prefusioncat_t_kernel(
+    tc,
+    img_feat0, img_feat1, img_feat2, img_feat3, img_feat4, pts_feat0,
+    img_w, img_b, img_gamma, img_beta, img_mean, img_var,
+    pts_w, pts_b, pts_gamma, pts_beta, pts_mean, pts_var,
+    out,
+):
+    nc = tc.nc
+    with ExitStack() as ctx:
+        const = ctx.enter_context(tc.tile_pool(name="const", bufs=1))
+        big = ctx.enter_context(tc.tile_pool(name="big", bufs=8))
+        grp = ctx.enter_context(tc.tile_pool(name="grp", bufs=5))
+        cod = ctx.enter_context(tc.tile_pool(name="cod", bufs=3))
+        psum = ctx.enter_context(tc.psum_pool(name="psum", bufs=2))
+
+        eps = const.tile([P, 1], F32, name="eps")
+        junk = const.tile([P, 1], F32, name="junk")
+        nc.vector.memset(eps[:], BN_EPS)
+        nc.scalar.activation(out=junk[:], in_=eps[:], func=ACT.Sqrt)
+        ident = const.tile([P, P], F32, name="ident")
+        masks.make_identity(nc, ident[:])
+
+        def level_view(feat):
+            return feat.rearrange("n (g p j) h w -> p (n g) (j h w)", g=G, p=P, j=J)
+
+        f1 = const.tile([P, NS * G, J * 128], BF16, name="f1")
+        f2 = const.tile([P, NS * G, J * 32], BF16, name="f2")
+        f3 = const.tile([P, NS * G, J * 8], BF16, name="f3")
+        f4 = const.tile([P, NS * G, J * 2], BF16, name="f4")
+        wraw = big.tile([P, 2, MT, 1024], BF16, name="wraw", tag="big")
+        f0 = big.tile([P, NS * G, J * 512], BF16, name="f0", tag="big")
+        wide = big.tile([P, NS * G * J, 8, CW], F32, name="wide", tag="big")
+        bn = const.tile([P, 5, 2, 16], BF16, name="bn")
+        raw = {}
+        for n in range(NS):
+            for g in range(G):
+                raw[(n, g)] = big.tile([P, J, HW], BF16, name="raw%d%d" % (n, g), tag="big")
+        pts_view = pts_feat0.rearrange("n (g p j) h w -> n g p (j h w)", g=G, p=P, j=J)
+
+        def load_raw(n, g):
+            nc.sync.dma_start(out=raw[(n, g)][:].rearrange("p j x -> p (j x)"), in_=pts_view[n, g])
+
+        def load_bn(kind, br, vec):
+            nc.scalar.dma_start(out=bn[:, kind, br, 0:MT], in_=vec.rearrange("(p m) -> p m", m=MT))
+
+        nc.sync.dma_start(out=f1[:], in_=level_view(img_feat1))
+        nc.sync.dma_start(out=f2[:], in_=level_view(img_feat2))
+        nc.sync.dma_start(out=f3[:], in_=level_view(img_feat3))
+        nc.sync.dma_start(out=f4[:], in_=level_view(img_feat4))
+        nc.sync.dma_start(out=wraw[:, 0].rearrange("p m c -> p (m c)"), in_=img_w.rearrange("(p m) c -> p (m c)", m=MT))
+        nc.sync.dma_start(out=f0[:], in_=level_view(img_feat0))
+        nc.sync.dma_start(out=wraw[:, 1].rearrange("p m c -> p (m c)"), in_=pts_w.rearrange("(p m) c -> p (m c)", m=MT))
+        load_bn(4, 0, img_var)
+        load_bn(4, 1, pts_var)
+        load_bn(1, 0, img_gamma)
+        load_bn(0, 0, img_b)
+        load_bn(3, 0, img_mean)
+        load_raw(0, 0)
+        load_raw(0, 1)
+        load_raw(1, 0)
+        load_bn(2, 0, img_beta)
+        load_bn(1, 1, pts_gamma)
+        load_bn(0, 1, pts_b)
+        load_bn(3, 1, pts_mean)
+        load_bn(2, 1, pts_beta)
+        load_raw(1, 1)
+
+        std = const.tile([P, 2, MT], F32, name="std")
+        rstd = const.tile([P, 2, MT], F32, name="rstd")
+        scl = const.tile([P, 2, MT], F32, name="scl")
+        dif = const.tile([P, 2, MT], F32, name="dif")
+        prod = const.tile([P, 2, MT], F32, name="prod")
+        shf = const.tile([P, 2, MT], F32, name="shf")
+        nc.scalar.activation(out=std[:], in_=bn[:, 4, :, 0:MT], func=ACT.Sqrt, bias=eps[:, 0:1], scale=1.0)
+
+        def bn_params():
+            nc.vector.reciprocal(out=rstd[:], in_=std[:])
+            nc.vector.tensor_tensor(out=scl[:], in0=bn[:, 1, :, 0:MT], in1=rstd[:], op=ALU.mult)
+            nc.vector.tensor_tensor(out=dif[:], in0=bn[:, 0, :, 0:MT], in1=bn[:, 3, :, 0:MT], op=ALU.subtract)
+            nc.vector.tensor_tensor(out=prod[:], in0=dif[:], in1=scl[:], op=ALU.mult)
+            nc.vector.tensor_tensor(out=shf[:], in0=prod[:], in1=bn[:, 2, :, 0:MT], op=ALU.add)
+
+        NC16 = NS * G * J
+        f1v = f1[:].rearrange("p a (j h w) -> p (a j) h w", j=J, h=8, w=16)
+        f2v = f2[:].rearrange("p a (j h w) -> p (a j) h w", j=J, h=4, w=8)
+        f3v = f3[:].rearrange("p a (j h w) -> p (a j) h w", j=J, h=2, w=4)
+        f4v = f4[:].rearrange("p a (j w) -> p (a j) w", j=J, w=2)
+        s3 = const.tile([P, NC16, 2, 4], F32, name="s3")
+        s2 = const.tile([P, NC16, 4, 8], F32, name="s2")
+        s1 = const.tile([P, NC16, 8, 16], F32, name="s1")
+        for h in range(2):
+            nc.vector.tensor_tensor(
+                out=s3[:, :, h, :].rearrange("p c (a b) -> p c a b", b=2),
+                in0=f3v[:, :, h, :].rearrange("p c (a b) -> p c a b", b=2),
+                in1=f4v.unsqueeze(3).to_broadcast([P, NC16, 2, 2]),
+                op=ALU.add,
+            )
+
+        def pad_add(dst, fine, coarse, hi, wi):
+            for r0, r1, a0, a1 in spans(hi):
+                for c0, c1, b0, b1 in spans(wi):
+                    nc.vector.tensor_tensor(
+                        out=dst[:, :, r0:r1, c0:c1],
+                        in0=fine[:, :, r0:r1, c0:c1],
+                        in1=coarse[:, :, a0:a1, b0:b1].to_broadcast([P, NC16, r1 - r0, c1 - c0]),
+                        op=ALU.add,
+                    )
+
+        pad_add(s2, f2v, s3, 2, 4)
+        pad_add(s1, f1v, s2, 4, 8)
+
+        HALF = G * J
+        for c0, c1, b0, b1 in spans(16):
+            nc.vector.tensor_copy(
+                out=wide[:, 0:HALF, :, c0:c1],
+                in_=s1[:, 0:HALF, :, b0:b1].to_broadcast([P, HALF, 8, c1 - c0]),
+            )
+        nc.scalar.copy(
+            out=wide[:, HALF:NC16].rearrange("p c h (w r) -> p (c h w) r", r=2),
+            in_=s1[:, HALF:NC16].rearrange("p c h w -> p (c h w)").unsqueeze(2).to_broadcast([P, HALF * 128, 2]),
+        )
+
+        w32 = wraw[:].bitcast(F32)
+        wc, ws = [], []
+        for br in range(2):
+            wc.append(const.tile([P, G * 512], U32, name="wc%d" % br, align_bytes=64))
+            ws.append(const.tile([P, G * 512], U8, name="ws%d" % br, align_bytes=64))
+
+        def weights(br):
+            wgrp = const.tile([P, G, 512, J], BF16, name="wgrp%d" % br, tag="wgrp", align_bytes=64)
+            wg32 = wgrp[:].bitcast(F32)
+            for g in range(G):
+                for mp in range(2):
+                    tp = psum.tile([P, 2, 2, P], F32, name="tp", tag="tp")
+                    for u in range(2):
+                        for mm in range(2):
+                            nc.tensor.transpose(
+                                tp[:, u, mm, :],
+                                w32[:, br, 2 * mp + mm, 256 * g + u : 256 * (g + 1) : 2],
+                                ident[:],
+                            )
+                    nc.scalar.copy(
+                        out=wg32[:, g, 256 * mp : 256 * (mp + 1), :],
+                        in_=tp[:].rearrange("p u m o -> p (m o) u"),
+                    )
+            nc.vector.quantize_mx(
+                out=wc[br][:].bitcast(FP8X4),
+                scales=ws[br][:],
+                in_=wgrp[:].rearrange("p g o t -> p (g o t)"),
+            )
+
+        weights(0)
+
+        def quantise(src, codes, scales):
+            nc.vector.quantize_mx(
+                out=codes[:].rearrange("p g x -> p (g x)").bitcast(FP8X4),
+                scales=scales[:].rearrange("p g x -> p (g x)"),
+                in_=src[:].rearrange("p g x t -> p (g x t)"),
+            )
+
+        def passes(acc, br, m, codes, scales):
+            for g in range(G):
+                cols = slice(512 * g + P * m, 512 * g + P * (m + 1))
+                nc.tensor.matmul_mx(
+                    out=acc[:],
+                    lhsT=wc[br][:, cols].bitcast(FP8X4),
+                    lhsT_scale=ws[br][:, cols],
+                    rhs=codes[:, g, :].bitcast(FP8X4),
+                    rhs_scale=scales[:, g, :],
+                    start=(g == 0),
+                    stop=(g == G - 1),
+                )
+
+        f0v = f0[:].rearrange("p a (j h w) -> p a j h w", j=J, h=CH, w=CW)
+        icod, isca = [], []
+        for n in range(NS):
+            icod.append(const.tile([P, G, 512], U32, name="icod%d" % n, align_bytes=64))
+            isca.append(const.tile([P, G, 512], U8, name="isca%d" % n, align_bytes=64))
+
+        def image_sum(n):
+            gi = grp.tile([P, G, 512, J], BF16, name="gi%d" % n, tag="grp", align_bytes=64)
+            for g in range(G):
+                a = n * G + g
+                dst = gi[:, g].rearrange("p (h w) j -> p h w j", w=CW)
+                fine = f0v[:, a].rearrange("p j h w -> p h w j")
+                coarse = wide[:, a * J : (a + 1) * J].rearrange("p j h w -> p h w j")
+                if n == 0:
+                    for r0, r1, a0, a1 in spans(8):
+                        nc.vector.tensor_tensor(
+                            out=dst[:, r0:r1],
+                            in0=fine[:, r0:r1],
+                            in1=coarse[:, a0:a1].to_broadcast([P, r1 - r0, CW, J]),
+                            op=ALU.add,
+                        )
+                else:
+                    for r in range(2):
+                        nc.vector.tensor_tensor(
+                            out=dst[:, r:CH:2], in0=fine[:, r:CH:2], in1=coarse, op=ALU.add
+                        )
+            quantise(gi, icod[n], isca[n])
+
+        out_view = out.rearrange("n (b p m) h w -> n b p m (h w)", b=2, p=P, m=MT)
+
+        def image_out(n, mp):
+            ist = big.tile([P, 2, 32, 64], F32, name="ist%d%d" % (n, mp), tag="big")
+            for mm in range(2):
+                m = 2 * mp + mm
+                acc = psum.tile([P, 512], F32, name="acc", tag="acc", bufs=6)
+                passes(acc, 0, m, icod[n], isca[n])
+                nc.scalar.activation(
+                    out=ist[:, mm, 8:24, 16:48],
+                    in_=acc[:].rearrange("p (h w) -> p h w", w=CW),
+                    func=ACT.Relu,
+                    bias=shf[:, 0, m : m + 1],
+                    scale=scl[:, 0, m : m + 1],
+                )
+            nc.vector.tensor_copy(out=ist[:, :, 8:24, 0:16], in_=ist[:, :, 8:24, 16:17].to_broadcast([P, 2, 16, 16]))
+            nc.vector.tensor_copy(out=ist[:, :, 8:24, 48:64], in_=ist[:, :, 8:24, 47:48].to_broadcast([P, 2, 16, 16]))
+            nc.vector.tensor_copy(out=ist[:, :, 0:8, :], in_=ist[:, :, 8:9, :].to_broadcast([P, 2, 8, 64]))
+            nc.vector.tensor_copy(out=ist[:, :, 24:32, :], in_=ist[:, :, 23:24, :].to_broadcast([P, 2, 8, 64]))
+            nc.sync.dma_start(
+                out=out_view[n, 0, :, 2 * mp : 2 * mp + 2, :],
+                in_=ist[:].rearrange("p m h w -> p m (h w)"),
+            )
+
+        image_sum(0)
+        bn_params()
+        weights(1)
+        image_out(0, 0)
+        image_out(0, 1)
+        image_sum(1)
+        image_out(1, 0)
+        image_out(1, 1)
+
+        pst = None
+        for n in range(NS):
+            for q in range(NQ):
+                gp = grp.tile([P, G, 512, J], BF16, name="gp%d%d" % (n, q), tag="grp", align_bytes=64)
+                for g in range(G):
+                    copy = nc.scalar.copy if (n, g, q) in SCALAR_UNITS else nc.vector.tensor_copy
+                    copy(
+                        out=gp[:, g].rearrange("p (c i) t -> p c t i", i=4),
+                        in_=raw[(n, g)][:, :, 512 * q : 512 * (q + 1)].rearrange("p t (c i) -> p c t i", i=4),
+                    )
+                pcod = cod.tile([P, G, 512], U32, name="pcod", tag="pcod", align_bytes=64)
+                psca = cod.tile([P, G, 512], U8, name="psca", tag="psca", align_bytes=64)
+                quantise(gp, pcod, psca)
+                if q % 2 == 0:
+                    pst = big.tile([P, MT, 1024], F32, name="pst%d%d" % (n, q // 2), tag="big")
+                for m in range(MT):
+                    acc = psum.tile([P, 512], F32, name="acc", tag="acc", bufs=6)
+                    passes(acc, 1, m, pcod, psca)
+                    nc.scalar.activation(
+                        out=pst[:, m, 512 * (q % 2) : 512 * (q % 2 + 1)],
+                        in_=acc[:],
+                        func=ACT.Relu,
+                        bias=shf[:, 1, m : m + 1],
+                        scale=scl[:, 1, m : m + 1],
+                    )
+                if q % 2 == 1:
+                    half = q // 2
+                    nc.sync.dma_start(out=out_view[n, 1, :, :, 1024 * half : 1024 * (half + 1)], in_=pst[:])

@@ -23,7 +23,8 @@ BN_EPS = 1e-5
 
 FLOPS = 2 * 2 * NS * 512 * 1024 * HW
 
-SCALAR_UNITS = ((0, 0, 0), (0, 0, 1), (0, 0, 2), (0, 0, 3), (1, 0, 0), (1, 0, 1))
+MANUAL = True
+SCALAR_UNITS = ((0, 0, 0), (0, 0, 1), (0, 0, 2), (0, 0, 3), (1, 0, 3))
 
 
 def spans(inner):
@@ -40,6 +41,8 @@ def tile_prefusioncat_t_kernel(
 ):
     nc = tc.nc
     with ExitStack() as ctx:
+        if MANUAL:
+            ctx.enter_context(tc.manual_schedule())
         const = ctx.enter_context(tc.tile_pool(name="const", bufs=1))
         big = ctx.enter_context(tc.tile_pool(name="big", bufs=8))
         grp = ctx.enter_context(tc.tile_pool(name="grp", bufs=5))
@@ -60,10 +63,10 @@ def tile_prefusioncat_t_kernel(
         f2 = const.tile([P, NS * G, J * 32], BF16, name="f2")
         f3 = const.tile([P, NS * G, J * 8], BF16, name="f3")
         f4 = const.tile([P, NS * G, J * 2], BF16, name="f4")
-        wraw = big.tile([P, 2, MT, 1024], BF16, name="wraw", tag="big")
         f0 = big.tile([P, NS * G, J * 512], BF16, name="f0", tag="big")
+        wraw = big.tile([P, 2, MT, 1024], BF16, name="wraw", tag="big")
         wide = big.tile([P, NS * G * J, 8, CW], F32, name="wide", tag="big")
-        bn = const.tile([P, 5, 2, 16], BF16, name="bn")
+        bn = const.tile([P, 2, 5, 16], BF16, name="bn")
         raw = {}
         for n in range(NS):
             for g in range(G):
@@ -73,47 +76,50 @@ def tile_prefusioncat_t_kernel(
         def load_raw(n, g):
             nc.sync.dma_start(out=raw[(n, g)][:].rearrange("p j x -> p (j x)"), in_=pts_view[n, g])
 
-        def load_bn(kind, br, vec):
-            nc.scalar.dma_start(out=bn[:, kind, br, 0:MT], in_=vec.rearrange("(p m) -> p m", m=MT))
+        def load_bn(br, vecs):
+            for kind, vec in enumerate(vecs):
+                nc.sync.dma_start(out=bn[:, br, kind, 0:MT], in_=vec.rearrange("(p m) -> p m", m=MT))
+
+        def load_w(br, w):
+            nc.sync.dma_start(out=wraw[:, br].rearrange("p m c -> p (m c)"), in_=w.rearrange("(p m) c -> p (m c)", m=MT))
 
         nc.sync.dma_start(out=f1[:], in_=level_view(img_feat1))
         nc.sync.dma_start(out=f2[:], in_=level_view(img_feat2))
         nc.sync.dma_start(out=f3[:], in_=level_view(img_feat3))
         nc.sync.dma_start(out=f4[:], in_=level_view(img_feat4))
-        nc.sync.dma_start(out=wraw[:, 0].rearrange("p m c -> p (m c)"), in_=img_w.rearrange("(p m) c -> p (m c)", m=MT))
         nc.sync.dma_start(out=f0[:], in_=level_view(img_feat0))
-        nc.sync.dma_start(out=wraw[:, 1].rearrange("p m c -> p (m c)"), in_=pts_w.rearrange("(p m) c -> p (m c)", m=MT))
-        load_bn(4, 0, img_var)
-        load_bn(4, 1, pts_var)
-        load_bn(1, 0, img_gamma)
-        load_bn(0, 0, img_b)
-        load_bn(3, 0, img_mean)
+        load_w(0, img_w)
+        load_bn(0, (img_var, img_gamma, img_b, img_mean, img_beta))
+        load_w(1, pts_w)
         load_raw(0, 0)
         load_raw(0, 1)
+        load_bn(1, (pts_var, pts_gamma, pts_b, pts_mean, pts_beta))
         load_raw(1, 0)
-        load_bn(2, 0, img_beta)
-        load_bn(1, 1, pts_gamma)
-        load_bn(0, 1, pts_b)
-        load_bn(3, 1, pts_mean)
-        load_bn(2, 1, pts_beta)
         load_raw(1, 1)
 
-        std = const.tile([P, 2, MT], F32, name="std")
-        rstd = const.tile([P, 2, MT], F32, name="rstd")
-        scl = const.tile([P, 2, MT], F32, name="scl")
-        dif = const.tile([P, 2, MT], F32, name="dif")
-        prod = const.tile([P, 2, MT], F32, name="prod")
-        shf = const.tile([P, 2, MT], F32, name="shf")
-        nc.scalar.activation(out=std[:], in_=bn[:, 4, :, 0:MT], func=ACT.Sqrt, bias=eps[:, 0:1], scale=1.0)
+        bnt = {}
+        for br in range(2):
+            for nm in ("std", "rstd", "scl", "dif", "prod", "shf"):
+                bnt[(nm, br)] = const.tile([P, MT], F32, name="%s%d" % (nm, br))
 
-        def bn_params():
-            nc.vector.reciprocal(out=rstd[:], in_=std[:])
-            nc.vector.tensor_tensor(out=scl[:], in0=bn[:, 1, :, 0:MT], in1=rstd[:], op=ALU.mult)
-            nc.vector.tensor_tensor(out=dif[:], in0=bn[:, 0, :, 0:MT], in1=bn[:, 3, :, 0:MT], op=ALU.subtract)
-            nc.vector.tensor_tensor(out=prod[:], in0=dif[:], in1=scl[:], op=ALU.mult)
-            nc.vector.tensor_tensor(out=shf[:], in0=prod[:], in1=bn[:, 2, :, 0:MT], op=ALU.add)
+        def bn_sqrt(br):
+            nc.scalar.activation(out=bnt[("std", br)][:], in_=bn[:, br, 0, 0:MT], func=ACT.Sqrt, bias=eps[:, 0:1], scale=1.0)
+
+        def bn_params(br):
+            nc.vector.reciprocal(out=bnt[("rstd", br)][:], in_=bnt[("std", br)][:])
+            nc.vector.tensor_tensor(out=bnt[("scl", br)][:], in0=bn[:, br, 1, 0:MT], in1=bnt[("rstd", br)][:], op=ALU.mult)
+            nc.vector.tensor_tensor(out=bnt[("dif", br)][:], in0=bn[:, br, 2, 0:MT], in1=bn[:, br, 3, 0:MT], op=ALU.subtract)
+            nc.vector.tensor_tensor(out=bnt[("prod", br)][:], in0=bnt[("dif", br)][:], in1=bnt[("scl", br)][:], op=ALU.mult)
+            nc.vector.tensor_tensor(out=bnt[("shf", br)][:], in0=bnt[("prod", br)][:], in1=bn[:, br, 4, 0:MT], op=ALU.add)
+
+        def bn_relu(dst, src, br, m):
+            nc.scalar.activation(
+                out=dst, in_=src, func=ACT.Relu,
+                bias=bnt[("shf", br)][:, m : m + 1], scale=bnt[("scl", br)][:, m : m + 1],
+            )
 
         NC16 = NS * G * J
+        HALF = G * J
         f1v = f1[:].rearrange("p a (j h w) -> p (a j) h w", j=J, h=8, w=16)
         f2v = f2[:].rearrange("p a (j h w) -> p (a j) h w", j=J, h=4, w=8)
         f3v = f3[:].rearrange("p a (j h w) -> p (a j) h w", j=J, h=2, w=4)
@@ -121,13 +127,6 @@ def tile_prefusioncat_t_kernel(
         s3 = const.tile([P, NC16, 2, 4], F32, name="s3")
         s2 = const.tile([P, NC16, 4, 8], F32, name="s2")
         s1 = const.tile([P, NC16, 8, 16], F32, name="s1")
-        for h in range(2):
-            nc.vector.tensor_tensor(
-                out=s3[:, :, h, :].rearrange("p c (a b) -> p c a b", b=2),
-                in0=f3v[:, :, h, :].rearrange("p c (a b) -> p c a b", b=2),
-                in1=f4v.unsqueeze(3).to_broadcast([P, NC16, 2, 2]),
-                op=ALU.add,
-            )
 
         def pad_add(dst, fine, coarse, hi, wi):
             for r0, r1, a0, a1 in spans(hi):
@@ -139,29 +138,39 @@ def tile_prefusioncat_t_kernel(
                         op=ALU.add,
                     )
 
-        pad_add(s2, f2v, s3, 2, 4)
-        pad_add(s1, f1v, s2, 4, 8)
+        def pyramid():
+            for h in range(2):
+                nc.vector.tensor_tensor(
+                    out=s3[:, :, h, :].rearrange("p c (a b) -> p c a b", b=2),
+                    in0=f3v[:, :, h, :].rearrange("p c (a b) -> p c a b", b=2),
+                    in1=f4v.unsqueeze(3).to_broadcast([P, NC16, 2, 2]),
+                    op=ALU.add,
+                )
+            pad_add(s2, f2v, s3, 2, 4)
+            pad_add(s1, f1v, s2, 4, 8)
 
-        HALF = G * J
-        for c0, c1, b0, b1 in spans(16):
-            nc.vector.tensor_copy(
-                out=wide[:, 0:HALF, :, c0:c1],
-                in_=s1[:, 0:HALF, :, b0:b1].to_broadcast([P, HALF, 8, c1 - c0]),
+        def widen0():
+            for c0, c1, b0, b1 in spans(16):
+                nc.vector.tensor_copy(
+                    out=wide[:, 0:HALF, :, c0:c1],
+                    in_=s1[:, 0:HALF, :, b0:b1].to_broadcast([P, HALF, 8, c1 - c0]),
+                )
+
+        def widen1():
+            nc.scalar.copy(
+                out=wide[:, HALF:NC16].rearrange("p c h (w r) -> p (c h w) r", r=2),
+                in_=s1[:, HALF:NC16].rearrange("p c h w -> p (c h w)").unsqueeze(2).to_broadcast([P, HALF * 128, 2]),
             )
-        nc.scalar.copy(
-            out=wide[:, HALF:NC16].rearrange("p c h (w r) -> p (c h w) r", r=2),
-            in_=s1[:, HALF:NC16].rearrange("p c h w -> p (c h w)").unsqueeze(2).to_broadcast([P, HALF * 128, 2]),
-        )
 
         w32 = wraw[:].bitcast(F32)
-        wc, ws = [], []
+        wc, ws, wgrp = [], [], {}
         for br in range(2):
             wc.append(const.tile([P, G * 512], U32, name="wc%d" % br, align_bytes=64))
             ws.append(const.tile([P, G * 512], U8, name="ws%d" % br, align_bytes=64))
 
-        def weights(br):
-            wgrp = const.tile([P, G, 512, J], BF16, name="wgrp%d" % br, tag="wgrp", align_bytes=64)
-            wg32 = wgrp[:].bitcast(F32)
+        def w_transposes(br):
+            wgrp[br] = const.tile([P, G, 512, J], BF16, name="wgrp%d" % br, tag="wgrp", align_bytes=64)
+            wg32 = wgrp[br][:].bitcast(F32)
             for g in range(G):
                 for mp in range(2):
                     tp = psum.tile([P, 2, 2, P], F32, name="tp", tag="tp")
@@ -176,13 +185,13 @@ def tile_prefusioncat_t_kernel(
                         out=wg32[:, g, 256 * mp : 256 * (mp + 1), :],
                         in_=tp[:].rearrange("p u m o -> p (m o) u"),
                     )
+
+        def w_quant(br):
             nc.vector.quantize_mx(
                 out=wc[br][:].bitcast(FP8X4),
                 scales=ws[br][:],
-                in_=wgrp[:].rearrange("p g o t -> p (g o t)"),
+                in_=wgrp[br][:].rearrange("p g o t -> p (g o t)"),
             )
-
-        weights(0)
 
         def quantise(src, codes, scales):
             nc.vector.quantize_mx(
@@ -191,7 +200,8 @@ def tile_prefusioncat_t_kernel(
                 in_=src[:].rearrange("p g x t -> p (g x t)"),
             )
 
-        def passes(acc, br, m, codes, scales):
+        def passes(br, m, codes, scales):
+            acc = psum.tile([P, 512], F32, name="acc", tag="acc", bufs=6)
             for g in range(G):
                 cols = slice(512 * g + P * m, 512 * g + P * (m + 1))
                 nc.tensor.matmul_mx(
@@ -203,93 +213,160 @@ def tile_prefusioncat_t_kernel(
                     start=(g == 0),
                     stop=(g == G - 1),
                 )
+            return acc
 
         f0v = f0[:].rearrange("p a (j h w) -> p a j h w", j=J, h=CH, w=CW)
-        icod, isca = [], []
+        icod, isca, gi = [], [], {}
         for n in range(NS):
             icod.append(const.tile([P, G, 512], U32, name="icod%d" % n, align_bytes=64))
             isca.append(const.tile([P, G, 512], U8, name="isca%d" % n, align_bytes=64))
 
-        def image_sum(n):
-            gi = grp.tile([P, G, 512, J], BF16, name="gi%d" % n, tag="grp", align_bytes=64)
-            for g in range(G):
-                a = n * G + g
-                dst = gi[:, g].rearrange("p (h w) j -> p h w j", w=CW)
-                fine = f0v[:, a].rearrange("p j h w -> p h w j")
-                coarse = wide[:, a * J : (a + 1) * J].rearrange("p j h w -> p h w j")
-                if n == 0:
-                    for r0, r1, a0, a1 in spans(8):
-                        nc.vector.tensor_tensor(
-                            out=dst[:, r0:r1],
-                            in0=fine[:, r0:r1],
-                            in1=coarse[:, a0:a1].to_broadcast([P, r1 - r0, CW, J]),
-                            op=ALU.add,
-                        )
-                else:
-                    for r in range(2):
-                        nc.vector.tensor_tensor(
-                            out=dst[:, r:CH:2], in0=fine[:, r:CH:2], in1=coarse, op=ALU.add
-                        )
-            quantise(gi, icod[n], isca[n])
+        def img_sum(n, g):
+            if g == 0:
+                gi[n] = grp.tile([P, G, 512, J], BF16, name="gi%d" % n, tag="grp", align_bytes=64)
+            a = n * G + g
+            dst = gi[n][:, g].rearrange("p (h w) j -> p h w j", w=CW)
+            fine = f0v[:, a].rearrange("p j h w -> p h w j")
+            coarse = wide[:, a * J : (a + 1) * J].rearrange("p j h w -> p h w j")
+            if n == 0:
+                for r0, r1, a0, a1 in spans(8):
+                    nc.vector.tensor_tensor(
+                        out=dst[:, r0:r1],
+                        in0=fine[:, r0:r1],
+                        in1=coarse[:, a0:a1].to_broadcast([P, r1 - r0, CW, J]),
+                        op=ALU.add,
+                    )
+            else:
+                for r in range(2):
+                    nc.vector.tensor_tensor(out=dst[:, r:CH:2], in0=fine[:, r:CH:2], in1=coarse, op=ALU.add)
+
+        def img_quant(n):
+            quantise(gi[n], icod[n], isca[n])
 
         out_view = out.rearrange("n (b p m) h w -> n b p m (h w)", b=2, p=P, m=MT)
+        ist, iacc = {}, {}
 
-        def image_out(n, mp):
-            ist = big.tile([P, 2, 32, 64], F32, name="ist%d%d" % (n, mp), tag="big")
+        def img_mm(k):
+            n, mp = divmod(k, 2)
             for mm in range(2):
-                m = 2 * mp + mm
-                acc = psum.tile([P, 512], F32, name="acc", tag="acc", bufs=6)
-                passes(acc, 0, m, icod[n], isca[n])
-                nc.scalar.activation(
-                    out=ist[:, mm, 8:24, 16:48],
-                    in_=acc[:].rearrange("p (h w) -> p h w", w=CW),
-                    func=ACT.Relu,
-                    bias=shf[:, 0, m : m + 1],
-                    scale=scl[:, 0, m : m + 1],
-                )
-            nc.vector.tensor_copy(out=ist[:, :, 8:24, 0:16], in_=ist[:, :, 8:24, 16:17].to_broadcast([P, 2, 16, 16]))
-            nc.vector.tensor_copy(out=ist[:, :, 8:24, 48:64], in_=ist[:, :, 8:24, 47:48].to_broadcast([P, 2, 16, 16]))
-            nc.vector.tensor_copy(out=ist[:, :, 0:8, :], in_=ist[:, :, 8:9, :].to_broadcast([P, 2, 8, 64]))
-            nc.vector.tensor_copy(out=ist[:, :, 24:32, :], in_=ist[:, :, 23:24, :].to_broadcast([P, 2, 8, 64]))
-            nc.sync.dma_start(
-                out=out_view[n, 0, :, 2 * mp : 2 * mp + 2, :],
-                in_=ist[:].rearrange("p m h w -> p m (h w)"),
+                iacc[(k, mm)] = passes(0, 2 * mp + mm, icod[n], isca[n])
+
+        def img_ev(k):
+            n, mp = divmod(k, 2)
+            ist[k] = big.tile([P, 2, 32, 64], F32, name="ist%d" % k, tag="big")
+            for mm in range(2):
+                bn_relu(ist[k][:, mm, 8:24, 16:48], iacc[(k, mm)][:].rearrange("p (h w) -> p h w", w=CW), 0, 2 * mp + mm)
+
+        def img_x(k):
+            n, mp = divmod(k, 2)
+            t = ist[k]
+            nc.vector.tensor_copy(out=t[:, :, 8:24, 0:16], in_=t[:, :, 8:24, 16:17].to_broadcast([P, 2, 16, 16]))
+            nc.vector.tensor_copy(out=t[:, :, 8:24, 48:64], in_=t[:, :, 8:24, 47:48].to_broadcast([P, 2, 16, 16]))
+            nc.vector.tensor_copy(out=t[:, :, 0:8, :], in_=t[:, :, 8:9, :].to_broadcast([P, 2, 8, 64]))
+            nc.vector.tensor_copy(out=t[:, :, 24:32, :], in_=t[:, :, 23:24, :].to_broadcast([P, 2, 8, 64]))
+            nc.sync.dma_start(out=out_view[n, 0, :, 2 * mp : 2 * mp + 2, :], in_=t[:].rearrange("p m h w -> p m (h w)"))
+
+        gp, pcod, psca, pacc, pst = {}, {}, {}, {}, {}
+
+        def regroup(n, g, q):
+            i = n * NQ + q
+            if i not in gp:
+                gp[i] = grp.tile([P, G, 512, J], BF16, name="gp%d" % i, tag="grp", align_bytes=64)
+            copy = nc.scalar.copy if (n, g, q) in SCALAR_UNITS else nc.vector.tensor_copy
+            copy(
+                out=gp[i][:, g].rearrange("p (c i) t -> p c t i", i=4),
+                in_=raw[(n, g)][:, :, 512 * q : 512 * (q + 1)].rearrange("p t (c i) -> p c t i", i=4),
             )
 
-        image_sum(0)
-        bn_params()
-        weights(1)
-        image_out(0, 0)
-        image_out(0, 1)
-        image_sum(1)
-        image_out(1, 0)
-        image_out(1, 1)
+        def pts_quant(i):
+            pcod[i] = cod.tile([P, G, 512], U32, name="pcod", tag="pcod", align_bytes=64)
+            psca[i] = cod.tile([P, G, 512], U8, name="psca", tag="psca", align_bytes=64)
+            quantise(gp[i], pcod[i], psca[i])
 
-        pst = None
-        for n in range(NS):
-            for q in range(NQ):
-                gp = grp.tile([P, G, 512, J], BF16, name="gp%d%d" % (n, q), tag="grp", align_bytes=64)
-                for g in range(G):
-                    copy = nc.scalar.copy if (n, g, q) in SCALAR_UNITS else nc.vector.tensor_copy
-                    copy(
-                        out=gp[:, g].rearrange("p (c i) t -> p c t i", i=4),
-                        in_=raw[(n, g)][:, :, 512 * q : 512 * (q + 1)].rearrange("p t (c i) -> p c t i", i=4),
-                    )
-                pcod = cod.tile([P, G, 512], U32, name="pcod", tag="pcod", align_bytes=64)
-                psca = cod.tile([P, G, 512], U8, name="psca", tag="psca", align_bytes=64)
-                quantise(gp, pcod, psca)
-                if q % 2 == 0:
-                    pst = big.tile([P, MT, 1024], F32, name="pst%d%d" % (n, q // 2), tag="big")
-                for m in range(MT):
-                    acc = psum.tile([P, 512], F32, name="acc", tag="acc", bufs=6)
-                    passes(acc, 1, m, pcod, psca)
-                    nc.scalar.activation(
-                        out=pst[:, m, 512 * (q % 2) : 512 * (q % 2 + 1)],
-                        in_=acc[:],
-                        func=ACT.Relu,
-                        bias=shf[:, 1, m : m + 1],
-                        scale=scl[:, 1, m : m + 1],
-                    )
-                if q % 2 == 1:
-                    half = q // 2
-                    nc.sync.dma_start(out=out_view[n, 1, :, :, 1024 * half : 1024 * (half + 1)], in_=pst[:])
+        def pts_mm(i):
+            for m in range(MT):
+                pacc[(i, m)] = passes(1, m, pcod[i], psca[i])
+
+        def pts_ev(i):
+            n, q = divmod(i, NQ)
+            half = q // 2
+            cols = slice(1024 * half, 1024 * (half + 1))
+            if q % 2 == 0:
+                pst[(n, half)] = big.tile([P, MT, 1024], F32, name="pst%d%d" % (n, half), tag="big")
+            t = pst[(n, half)]
+            for m in range(MT):
+                bn_relu(t[:, m, 512 * (q % 2) : 512 * (q % 2 + 1)], pacc[(i, m)][:], 1, m)
+                if i == NS * NQ - 1:
+                    nc.sync.dma_start(out=out_view[n, 1, :, m, cols], in_=t[:, m, :])
+            if q % 2 == 1 and i != NS * NQ - 1:
+                nc.sync.dma_start(out=out_view[n, 1, :, :, cols], in_=t[:])
+
+        pyramid()
+        widen0()
+        widen1()
+        bn_sqrt(0)
+        img_sum(0, 0)
+        img_sum(0, 1)
+        w_transposes(0)
+        w_quant(0)
+        img_quant(0)
+        bn_params(0)
+        w_transposes(1)
+        img_mm(0)
+        img_mm(1)
+        img_sum(1, 0)
+        img_ev(0)
+        img_ev(1)
+        img_x(0)
+        img_sum(1, 1)
+        img_x(1)
+        w_quant(1)
+        img_quant(1)
+        regroup(0, 0, 0)
+        regroup(0, 0, 1)
+        regroup(0, 0, 2)
+        regroup(0, 0, 3)
+        bn_sqrt(1)
+        img_mm(2)
+        img_mm(3)
+        regroup(0, 1, 0)
+        regroup(0, 1, 1)
+        bn_params(1)
+        pts_quant(0)
+        img_ev(2)
+        img_ev(3)
+        pts_mm(0)
+        regroup(0, 1, 2)
+        pts_quant(1)
+        img_x(2)
+        pts_ev(0)
+        pts_mm(1)
+        regroup(0, 1, 3)
+        pts_quant(2)
+        img_x(3)
+        pts_ev(1)
+        pts_mm(2)
+        regroup(1, 0, 0)
+        regroup(1, 1, 0)
+        pts_quant(3)
+        pts_ev(2)
+        regroup(1, 0, 3)
+        pts_mm(3)
+        regroup(1, 0, 1)
+        regroup(1, 1, 1)
+        pts_quant(4)
+        pts_ev(3)
+        pts_mm(4)
+        regroup(1, 0, 2)
+        regroup(1, 1, 2)
+        pts_quant(5)
+        pts_ev(4)
+        pts_mm(5)
+        pts_quant(6)
+        regroup(1, 1, 3)
+        pts_ev(5)
+        pts_mm(6)
+        pts_quant(7)
+        pts_ev(6)
+        pts_mm(7)
+        pts_ev(7)

@@ -23,7 +23,7 @@ BN_EPS = 1e-5
 
 FLOPS = 2 * 2 * NS * 512 * 1024 * HW
 
-MANUAL = True
+MANUAL = False
 SCALAR_UNITS = ((0, 0, 0), (0, 0, 1), (0, 0, 2), (0, 0, 3), (1, 0, 3))
 
 

@@ -23,8 +23,9 @@ BN_EPS = 1e-5
 
 FLOPS = 2 * 2 * NS * 512 * 1024 * HW
 
-MANUAL = False
-SCALAR_UNITS = ((0, 0, 0), (0, 0, 1), (0, 0, 2), (0, 0, 3), (1, 0, 3))
+MANUAL = True
+PAIRED = (0,)
+SCALAR_UNITS = ((0, 0, 0), (0, 0, 1), (0, 0, 2), (0, 0, 3), (0, 1, 0),)
 
 
 def spans(inner):
@@ -83,19 +84,14 @@ def tile_prefusioncat_t_kernel(
         def load_w(br, w):
             nc.sync.dma_start(out=wraw[:, br].rearrange("p m c -> p (m c)"), in_=w.rearrange("(p m) c -> p (m c)", m=MT))
 
-        nc.sync.dma_start(out=f1[:], in_=level_view(img_feat1))
-        nc.sync.dma_start(out=f2[:], in_=level_view(img_feat2))
-        nc.sync.dma_start(out=f3[:], in_=level_view(img_feat3))
-        nc.sync.dma_start(out=f4[:], in_=level_view(img_feat4))
-        nc.sync.dma_start(out=f0[:], in_=level_view(img_feat0))
-        load_w(0, img_w)
-        load_bn(0, (img_var, img_gamma, img_b, img_mean, img_beta))
-        load_w(1, pts_w)
-        load_raw(0, 0)
-        load_raw(0, 1)
-        load_bn(1, (pts_var, pts_gamma, pts_b, pts_mean, pts_beta))
-        load_raw(1, 0)
-        load_raw(1, 1)
+        def load_level(t, feat):
+            nc.sync.dma_start(out=t[:], in_=level_view(feat))
+
+        def load_f0(n):
+            nc.sync.dma_start(out=f0[:, G * n : G * (n + 1)], in_=level_view(img_feat0)[:, G * n : G * (n + 1)])
+
+        IMG_BN = (img_var, img_gamma, img_b, img_mean, img_beta)
+        PTS_BN = (pts_var, pts_gamma, pts_b, pts_mean, pts_beta)
 
         bnt = {}
         for br in range(2):
@@ -105,12 +101,17 @@ def tile_prefusioncat_t_kernel(
         def bn_sqrt(br):
             nc.scalar.activation(out=bnt[("std", br)][:], in_=bn[:, br, 0, 0:MT], func=ACT.Sqrt, bias=eps[:, 0:1], scale=1.0)
 
-        def bn_params(br):
-            nc.vector.reciprocal(out=bnt[("rstd", br)][:], in_=bnt[("std", br)][:])
-            nc.vector.tensor_tensor(out=bnt[("scl", br)][:], in0=bn[:, br, 1, 0:MT], in1=bnt[("rstd", br)][:], op=ALU.mult)
-            nc.vector.tensor_tensor(out=bnt[("dif", br)][:], in0=bn[:, br, 2, 0:MT], in1=bn[:, br, 3, 0:MT], op=ALU.subtract)
-            nc.vector.tensor_tensor(out=bnt[("prod", br)][:], in0=bnt[("dif", br)][:], in1=bnt[("scl", br)][:], op=ALU.mult)
-            nc.vector.tensor_tensor(out=bnt[("shf", br)][:], in0=bnt[("prod", br)][:], in1=bn[:, br, 4, 0:MT], op=ALU.add)
+        def bn_op(br, k):
+            if k == 0:
+                nc.vector.tensor_tensor(out=bnt[("dif", br)][:], in0=bn[:, br, 2, 0:MT], in1=bn[:, br, 3, 0:MT], op=ALU.subtract)
+            elif k == 1:
+                nc.vector.reciprocal(out=bnt[("rstd", br)][:], in_=bnt[("std", br)][:])
+            elif k == 2:
+                nc.vector.tensor_tensor(out=bnt[("scl", br)][:], in0=bn[:, br, 1, 0:MT], in1=bnt[("rstd", br)][:], op=ALU.mult)
+            elif k == 3:
+                nc.vector.tensor_tensor(out=bnt[("prod", br)][:], in0=bnt[("dif", br)][:], in1=bnt[("scl", br)][:], op=ALU.mult)
+            else:
+                nc.vector.tensor_tensor(out=bnt[("shf", br)][:], in0=bnt[("prod", br)][:], in1=bn[:, br, 4, 0:MT], op=ALU.add)
 
         def bn_relu(dst, src, br, m):
             nc.scalar.activation(
@@ -138,7 +139,7 @@ def tile_prefusioncat_t_kernel(
                         op=ALU.add,
                     )
 
-        def pyramid():
+        def level3():
             for h in range(2):
                 nc.vector.tensor_tensor(
                     out=s3[:, :, h, :].rearrange("p c (a b) -> p c a b", b=2),
@@ -146,7 +147,11 @@ def tile_prefusioncat_t_kernel(
                     in1=f4v.unsqueeze(3).to_broadcast([P, NC16, 2, 2]),
                     op=ALU.add,
                 )
+
+        def level2():
             pad_add(s2, f2v, s3, 2, 4)
+
+        def level1():
             pad_add(s1, f1v, s2, 4, 8)
 
         def widen0():
@@ -222,7 +227,7 @@ def tile_prefusioncat_t_kernel(
             isca.append(const.tile([P, G, 512], U8, name="isca%d" % n, align_bytes=64))
 
         def img_sum(n, g):
-            if g == 0:
+            if n not in gi:
                 gi[n] = grp.tile([P, G, 512, J], BF16, name="gi%d" % n, tag="grp", align_bytes=64)
             a = n * G + g
             dst = gi[n][:, g].rearrange("p (h w) j -> p h w j", w=CW)
@@ -257,11 +262,14 @@ def tile_prefusioncat_t_kernel(
             for mm in range(2):
                 bn_relu(ist[k][:, mm, 8:24, 16:48], iacc[(k, mm)][:].rearrange("p (h w) -> p h w", w=CW), 0, 2 * mp + mm)
 
-        def img_x(k):
-            n, mp = divmod(k, 2)
+        def img_xa(k):
             t = ist[k]
             nc.vector.tensor_copy(out=t[:, :, 8:24, 0:16], in_=t[:, :, 8:24, 16:17].to_broadcast([P, 2, 16, 16]))
             nc.vector.tensor_copy(out=t[:, :, 8:24, 48:64], in_=t[:, :, 8:24, 47:48].to_broadcast([P, 2, 16, 16]))
+
+        def img_xb(k):
+            n, mp = divmod(k, 2)
+            t = ist[k]
             nc.vector.tensor_copy(out=t[:, :, 0:8, :], in_=t[:, :, 8:9, :].to_broadcast([P, 2, 8, 64]))
             nc.vector.tensor_copy(out=t[:, :, 24:32, :], in_=t[:, :, 23:24, :].to_broadcast([P, 2, 8, 64]))
             nc.sync.dma_start(out=out_view[n, 0, :, 2 * mp : 2 * mp + 2, :], in_=t[:].rearrange("p m h w -> p m (h w)"))
@@ -289,6 +297,16 @@ def tile_prefusioncat_t_kernel(
 
         def pts_ev(i):
             n, q = divmod(i, NQ)
+            if n in PAIRED:
+                if q == 0:
+                    for mp in range(2):
+                        pst[(n, mp)] = big.tile([P, 2, HW], F32, name="pst%d%d" % (n, mp), tag="big")
+                for m in range(MT):
+                    bn_relu(pst[(n, m // 2)][:, m % 2, 512 * q : 512 * (q + 1)], pacc[(i, m)][:], 1, m)
+                    if q == NQ - 1 and m % 2 == 1:
+                        mp = m // 2
+                        nc.sync.dma_start(out=out_view[n, 1, :, 2 * mp : 2 * mp + 2, :], in_=pst[(n, mp)][:])
+                return
             half = q // 2
             cols = slice(1024 * half, 1024 * (half + 1))
             if q % 2 == 0:
@@ -301,65 +319,93 @@ def tile_prefusioncat_t_kernel(
             if q % 2 == 1 and i != NS * NQ - 1:
                 nc.sync.dma_start(out=out_view[n, 1, :, :, cols], in_=t[:])
 
-        pyramid()
+        load_level(f4, img_feat4)
+        load_level(f3, img_feat3)
+        load_level(f2, img_feat2)
+        load_level(f1, img_feat1)
+        load_f0(0)
+        load_bn(0, IMG_BN)
+        load_w(0, img_w)
+        load_f0(1)
+        load_w(1, pts_w)
+        load_raw(0, 0)
+        load_raw(0, 1)
+        load_bn(1, PTS_BN)
+        load_raw(1, 0)
+        load_raw(1, 1)
+        level3()
+        level2()
+        level1()
         widen0()
         widen1()
         bn_sqrt(0)
+        bn_op(0, 0)
         img_sum(0, 0)
         img_sum(0, 1)
         w_transposes(0)
         w_quant(0)
+        bn_op(0, 1)
         img_quant(0)
-        bn_params(0)
+        bn_op(0, 2)
+        bn_op(0, 3)
+        img_sum(1, 0)
+        bn_op(0, 4)
         w_transposes(1)
         img_mm(0)
+        regroup(0, 0, 0)
         img_mm(1)
-        img_sum(1, 0)
+        img_sum(1, 1)
         img_ev(0)
         img_ev(1)
-        img_x(0)
-        img_sum(1, 1)
-        img_x(1)
+        img_xa(0)
         w_quant(1)
+        img_xb(0)
+        img_xa(1)
         img_quant(1)
-        regroup(0, 0, 0)
         regroup(0, 0, 1)
-        regroup(0, 0, 2)
-        regroup(0, 0, 3)
+        img_xb(1)
         bn_sqrt(1)
         img_mm(2)
         img_mm(3)
         regroup(0, 1, 0)
+        regroup(0, 0, 2)
+        bn_op(1, 0)
+        bn_op(1, 1)
         regroup(0, 1, 1)
-        bn_params(1)
+        bn_op(1, 2)
         pts_quant(0)
+        bn_op(1, 3)
+        pts_quant(1)
+        bn_op(1, 4)
         img_ev(2)
+        regroup(0, 0, 3)
         img_ev(3)
         pts_mm(0)
+        img_xa(2)
         regroup(0, 1, 2)
-        pts_quant(1)
-        img_x(2)
+        img_xb(2)
         pts_ev(0)
         pts_mm(1)
-        regroup(0, 1, 3)
+        img_xa(3)
         pts_quant(2)
-        img_x(3)
+        regroup(0, 1, 3)
+        img_xb(3)
         pts_ev(1)
+        pts_quant(3)
         pts_mm(2)
+        pts_ev(2)
         regroup(1, 0, 0)
         regroup(1, 1, 0)
-        pts_quant(3)
-        pts_ev(2)
-        regroup(1, 0, 3)
-        pts_mm(3)
         regroup(1, 0, 1)
-        regroup(1, 1, 1)
+        pts_mm(3)
         pts_quant(4)
+        regroup(1, 1, 1)
+        regroup(1, 0, 2)
+        pts_quant(5)
         pts_ev(3)
         pts_mm(4)
-        regroup(1, 0, 2)
         regroup(1, 1, 2)
-        pts_quant(5)
+        regroup(1, 0, 3)
         pts_ev(4)
         pts_mm(5)
         pts_quant(6)

@@ -54,6 +54,10 @@ def tile_prefusioncat_t_kernel(
         junk = const.tile([P, 1], F32, name="junk")
         nc.vector.memset(eps[:], BN_EPS)
         nc.scalar.activation(out=junk[:], in_=eps[:], func=ACT.Sqrt)
+        bnrow = []
+        for br in range(2):
+            bnrow.append(const.tile([P, 512], BF16, name="bnrow%d" % br))
+            nc.gpsimd.memset(bnrow[br][:], 0.0)
         ident = const.tile([P, P], F32, name="ident")
         masks.make_identity(nc, ident[:])
 
@@ -67,7 +71,6 @@ def tile_prefusioncat_t_kernel(
         f0 = big.tile([P, NS * G, J * 512], BF16, name="f0", tag="big")
         wraw = big.tile([P, 2, MT, 1024], BF16, name="wraw", tag="big")
         wide = big.tile([P, NS * G * J, 8, CW], F32, name="wide", tag="big")
-        bn = const.tile([P, 2, 5, 16], BF16, name="bn")
         raw = {}
         for n in range(NS):
             for g in range(G):
@@ -79,7 +82,7 @@ def tile_prefusioncat_t_kernel(
 
         def load_bn(br, vecs):
             for kind, vec in enumerate(vecs):
-                nc.sync.dma_start(out=bn[:, br, kind, 0:MT], in_=vec.rearrange("(p m) -> p m", m=MT))
+                nc.sync.dma_start(out=bnrow[br][kind : kind + 1, :], in_=vec.rearrange("(a c) -> a c", a=1))
 
         def load_w(br, w):
             nc.sync.dma_start(out=wraw[:, br].rearrange("p m c -> p (m c)"), in_=w.rearrange("(p m) c -> p (m c)", m=MT))
@@ -98,20 +101,35 @@ def tile_prefusioncat_t_kernel(
             for nm in ("std", "rstd", "scl", "dif", "prod", "shf"):
                 bnt[(nm, br)] = const.tile([P, MT], F32, name="%s%d" % (nm, br))
 
+        bnp, bnf = {}, {}
+
+        def bn_turn(br):
+            words = bnrow[br][:].bitcast(F32)
+            bnp[br] = psum.tile([P, 2, P], F32, name="bnp", tag="tp")
+            for u in range(2):
+                nc.tensor.transpose(bnp[br][:, u, :], words[:, u:256:2], ident[:])
+
+        def bn_out(br):
+            bnf[br] = const.tile([P, 5, MT], F32, name="bnf%d" % br)
+            nc.vector.tensor_copy(
+                out=bnf[br][:].rearrange("p k (u e) -> p u k e", e=2),
+                in_=bnp[br][:].rearrange("p u r -> p (u r)").bitcast(BF16).rearrange("p (u r e) -> p u r e", u=2, e=2)[:, :, 0:5, :],
+            )
+
         def bn_sqrt(br):
-            nc.scalar.activation(out=bnt[("std", br)][:], in_=bn[:, br, 0, 0:MT], func=ACT.Sqrt, bias=eps[:, 0:1], scale=1.0)
+            nc.scalar.activation(out=bnt[("std", br)][:], in_=bnf[br][:, 0, :], func=ACT.Sqrt, bias=eps[:, 0:1], scale=1.0)
 
         def bn_op(br, k):
             if k == 0:
-                nc.vector.tensor_tensor(out=bnt[("dif", br)][:], in0=bn[:, br, 2, 0:MT], in1=bn[:, br, 3, 0:MT], op=ALU.subtract)
+                nc.vector.tensor_tensor(out=bnt[("dif", br)][:], in0=bnf[br][:, 2, :], in1=bnf[br][:, 3, :], op=ALU.subtract)
             elif k == 1:
                 nc.vector.reciprocal(out=bnt[("rstd", br)][:], in_=bnt[("std", br)][:])
             elif k == 2:
-                nc.vector.tensor_tensor(out=bnt[("scl", br)][:], in0=bn[:, br, 1, 0:MT], in1=bnt[("rstd", br)][:], op=ALU.mult)
+                nc.vector.tensor_tensor(out=bnt[("scl", br)][:], in0=bnf[br][:, 1, :], in1=bnt[("rstd", br)][:], op=ALU.mult)
             elif k == 3:
                 nc.vector.tensor_tensor(out=bnt[("prod", br)][:], in0=bnt[("dif", br)][:], in1=bnt[("scl", br)][:], op=ALU.mult)
             else:
-                nc.vector.tensor_tensor(out=bnt[("shf", br)][:], in0=bnt[("prod", br)][:], in1=bn[:, br, 4, 0:MT], op=ALU.add)
+                nc.vector.tensor_tensor(out=bnt[("shf", br)][:], in0=bnt[("prod", br)][:], in1=bnf[br][:, 4, :], op=ALU.add)
 
         def bn_relu(dst, src, br, m):
             nc.scalar.activation(
@@ -328,9 +346,9 @@ def tile_prefusioncat_t_kernel(
         load_w(0, img_w)
         load_f0(1)
         load_w(1, pts_w)
+        load_bn(1, PTS_BN)
         load_raw(0, 0)
         load_raw(0, 1)
-        load_bn(1, PTS_BN)
         load_raw(1, 0)
         load_raw(1, 1)
         level3()
@@ -338,6 +356,8 @@ def tile_prefusioncat_t_kernel(
         level1()
         widen0()
         widen1()
+        bn_turn(0)
+        bn_out(0)
         bn_sqrt(0)
         bn_op(0, 0)
         img_sum(0, 0)
@@ -351,6 +371,7 @@ def tile_prefusioncat_t_kernel(
         img_sum(1, 0)
         bn_op(0, 4)
         w_transposes(1)
+        bn_turn(1)
         img_mm(0)
         regroup(0, 0, 0)
         img_mm(1)
@@ -362,6 +383,7 @@ def tile_prefusioncat_t_kernel(
         img_xb(0)
         img_xa(1)
         img_quant(1)
+        bn_out(1)
         regroup(0, 0, 1)
         img_xb(1)
         bn_sqrt(1)

@@ -82,7 +82,7 @@ def tile_prefusioncat_t_kernel(
 
         def load_bn(br, vecs):
             for kind, vec in enumerate(vecs):
-                nc.sync.dma_start(out=bnrow[br][kind : kind + 1, :], in_=vec.rearrange("(a c) -> a c", a=1))
+                nc.gpsimd.dma_start(out=bnrow[br][kind : kind + 1, :], in_=vec.rearrange("(a c) -> a c", a=1))
 
         def load_w(br, w):
             nc.sync.dma_start(out=wraw[:, br].rearrange("p m c -> p (m c)"), in_=w.rearrange("(p m) c -> p (m c)", m=MT))
@@ -342,33 +342,33 @@ def tile_prefusioncat_t_kernel(
         load_level(f2, img_feat2)
         load_level(f1, img_feat1)
         load_f0(0)
-        load_bn(0, IMG_BN)
         load_w(0, img_w)
         load_f0(1)
         load_w(1, pts_w)
-        load_bn(1, PTS_BN)
         load_raw(0, 0)
         load_raw(0, 1)
         load_raw(1, 0)
         load_raw(1, 1)
+        load_bn(0, IMG_BN)
+        load_bn(1, PTS_BN)
         level3()
         level2()
         level1()
         widen0()
         widen1()
-        bn_turn(0)
-        bn_out(0)
-        bn_sqrt(0)
-        bn_op(0, 0)
         img_sum(0, 0)
         img_sum(0, 1)
         w_transposes(0)
+        bn_turn(0)
         w_quant(0)
-        bn_op(0, 1)
+        bn_out(0)
+        bn_sqrt(0)
         img_quant(0)
+        bn_op(0, 0)
+        bn_op(0, 1)
         bn_op(0, 2)
-        bn_op(0, 3)
         img_sum(1, 0)
+        bn_op(0, 3)
         bn_op(0, 4)
         w_transposes(1)
         bn_turn(1)

from contextlib import ExitStack

import concourse.masks as masks
import concourse.mybir as mybir

FP8X4 = mybir.dt.float8_e4m3fn_x4
BF16 = mybir.dt.bfloat16
F32 = mybir.dt.float32
U32 = mybir.dt.uint32
U8 = mybir.dt.uint8
ACT = mybir.ActivationFunctionType
ALU = mybir.AluOpType

P = 128
NS = 2
G = 2
J = 4
MT = 4
HW = 2048
NQ = 4
CH, CW = 16, 32
BN_EPS = 1e-5

FLOPS = 2 * 2 * NS * 512 * 1024 * HW

MANUAL = True
PAIRED = (0,)
SCALAR_UNITS = ((0, 0, 0), (0, 0, 1), (0, 0, 2), (0, 0, 3), (0, 1, 0),)


def spans(inner):
    off = inner // 2
    return ((0, off, 0, 1), (off, off + inner, 0, inner), (off + inner, 2 * inner, inner - 1, inner))


def tile_prefusioncat_t_kernel(
    tc,
    img_feat0, img_feat1, img_feat2, img_feat3, img_feat4, pts_feat0,
    img_w, img_b, img_gamma, img_beta, img_mean, img_var,
    pts_w, pts_b, pts_gamma, pts_beta, pts_mean, pts_var,
    out,
):
    nc = tc.nc
    with ExitStack() as ctx:
        if MANUAL:
            ctx.enter_context(tc.manual_schedule())
        const = ctx.enter_context(tc.tile_pool(name="const", bufs=1))
        big = ctx.enter_context(tc.tile_pool(name="big", bufs=8))
        grp = ctx.enter_context(tc.tile_pool(name="grp", bufs=5))
        cod = ctx.enter_context(tc.tile_pool(name="cod", bufs=3))
        psum = ctx.enter_context(tc.psum_pool(name="psum", bufs=2))

        eps = const.tile([P, 1], F32, name="eps")
        junk = const.tile([P, 1], F32, name="junk")
        nc.vector.memset(eps[:], BN_EPS)
        nc.scalar.activation(out=junk[:], in_=eps[:], func=ACT.Sqrt)
        bnrow = []
        for br in range(2):
            bnrow.append(const.tile([P, 512], BF16, name="bnrow%d" % br))
            nc.gpsimd.memset(bnrow[br][:], 0.0)
        ident = const.tile([P, P], F32, name="ident")
        masks.make_identity(nc, ident[:])

        def level_view(feat):
            return feat.rearrange("n (g p j) h w -> p (n g) (j h w)", g=G, p=P, j=J)

        f1 = const.tile([P, NS * G, J * 128], BF16, name="f1")
        f2 = const.tile([P, NS * G, J * 32], BF16, name="f2")
        f3 = const.tile([P, NS * G, J * 8], BF16, name="f3")
        f4 = const.tile([P, NS * G, J * 2], BF16, name="f4")
        f0 = big.tile([P, NS * G, J * 512], BF16, name="f0", tag="big")
        wraw = big.tile([P, 2, MT, 1024], BF16, name="wraw", tag="big")
        wide = big.tile([P, NS * G * J, 8, CW], F32, name="wide", tag="big")
        raw = {}
        for n in range(NS):
            for g in range(G):
                raw[(n, g)] = big.tile([P, J, HW], BF16, name="raw%d%d" % (n, g), tag="big")
        pts_view = pts_feat0.rearrange("n (g p j) h w -> n g p (j h w)", g=G, p=P, j=J)

        def load_raw(n, g):
            nc.sync.dma_start(out=raw[(n, g)][:].rearrange("p j x -> p (j x)"), in_=pts_view[n, g])

        def load_bn(br, vecs):
            for kind, vec in enumerate(vecs):
                nc.gpsimd.dma_start(out=bnrow[br][kind : kind + 1, :], in_=vec.rearrange("(a c) -> a c", a=1))

        def load_w(br, w):
            nc.sync.dma_start(out=wraw[:, br].rearrange("p m c -> p (m c)"), in_=w.rearrange("(p m) c -> p (m c)", m=MT))

        def load_level(t, feat):
            nc.sync.dma_start(out=t[:], in_=level_view(feat))

        def load_f0(n):
            nc.sync.dma_start(out=f0[:, G * n : G * (n + 1)], in_=level_view(img_feat0)[:, G * n : G * (n + 1)])

        IMG_BN = (img_var, img_gamma, img_b, img_mean, img_beta)
        PTS_BN = (pts_var, pts_gamma, pts_b, pts_mean, pts_beta)

        bnt = {}
        for br in range(2):
            for nm in ("std", "rstd", "scl", "dif", "prod", "shf"):
                bnt[(nm, br)] = const.tile([P, MT], F32, name="%s%d" % (nm, br))

        bnp, bnf = {}, {}

        def bn_turn(br):
            words = bnrow[br][:].bitcast(F32)
            bnp[br] = psum.tile([P, 2, P], F32, name="bnp", tag="tp")
            for u in range(2):
                nc.tensor.transpose(bnp[br][:, u, :], words[:, u:256:2], ident[:])

        def bn_out(br):
            bnf[br] = const.tile([P, 5, MT], F32, name="bnf%d" % br)
            nc.vector.tensor_copy(
                out=bnf[br][:].rearrange("p k (u e) -> p u k e", e=2),
                in_=bnp[br][:].rearrange("p u r -> p (u r)").bitcast(BF16).rearrange("p (u r e) -> p u r e", u=2, e=2)[:, :, 0:5, :],
            )

        def bn_sqrt(br):
            nc.scalar.activation(out=bnt[("std", br)][:], in_=bnf[br][:, 0, :], func=ACT.Sqrt, bias=eps[:, 0:1], scale=1.0)

        def bn_op(br, k):
            if k == 0:
                nc.vector.tensor_tensor(out=bnt[("dif", br)][:], in0=bnf[br][:, 2, :], in1=bnf[br][:, 3, :], op=ALU.subtract)
            elif k == 1:
                nc.vector.reciprocal(out=bnt[("rstd", br)][:], in_=bnt[("std", br)][:])
            elif k == 2:
                nc.vector.tensor_tensor(out=bnt[("scl", br)][:], in0=bnf[br][:, 1, :], in1=bnt[("rstd", br)][:], op=ALU.mult)
            elif k == 3:
                nc.vector.tensor_tensor(out=bnt[("prod", br)][:], in0=bnt[("dif", br)][:], in1=bnt[("scl", br)][:], op=ALU.mult)
            else:
                nc.vector.tensor_tensor(out=bnt[("shf", br)][:], in0=bnt[("prod", br)][:], in1=bnf[br][:, 4, :], op=ALU.add)

        def bn_relu(dst, src, br, m):
            nc.scalar.activation(
                out=dst, in_=src, func=ACT.Relu,
                bias=bnt[("shf", br)][:, m : m + 1], scale=bnt[("scl", br)][:, m : m + 1],
            )

        NC16 = NS * G * J
        HALF = G * J
        f1v = f1[:].rearrange("p a (j h w) -> p (a j) h w", j=J, h=8, w=16)
        f2v = f2[:].rearrange("p a (j h w) -> p (a j) h w", j=J, h=4, w=8)
        f3v = f3[:].rearrange("p a (j h w) -> p (a j) h w", j=J, h=2, w=4)
        f4v = f4[:].rearrange("p a (j w) -> p (a j) w", j=J, w=2)
        s3 = const.tile([P, NC16, 2, 4], F32, name="s3")
        s2 = const.tile([P, NC16, 4, 8], F32, name="s2")
        s1 = const.tile([P, NC16, 8, 16], F32, name="s1")

        def pad_add(dst, fine, coarse, hi, wi):
            for r0, r1, a0, a1 in spans(hi):
                for c0, c1, b0, b1 in spans(wi):
                    nc.vector.tensor_tensor(
                        out=dst[:, :, r0:r1, c0:c1],
                        in0=fine[:, :, r0:r1, c0:c1],
                        in1=coarse[:, :, a0:a1, b0:b1].to_broadcast([P, NC16, r1 - r0, c1 - c0]),
                        op=ALU.add,
                    )

        def level3():
            for h in range(2):
                nc.vector.tensor_tensor(
                    out=s3[:, :, h, :].rearrange("p c (a b) -> p c a b", b=2),
                    in0=f3v[:, :, h, :].rearrange("p c (a b) -> p c a b", b=2),
                    in1=f4v.unsqueeze(3).to_broadcast([P, NC16, 2, 2]),
                    op=ALU.add,
                )

        def level2():
            pad_add(s2, f2v, s3, 2, 4)

        def level1():
            pad_add(s1, f1v, s2, 4, 8)

        def widen0():
            for c0, c1, b0, b1 in spans(16):
                nc.vector.tensor_copy(
                    out=wide[:, 0:HALF, :, c0:c1],
                    in_=s1[:, 0:HALF, :, b0:b1].to_broadcast([P, HALF, 8, c1 - c0]),
                )

        def widen1():
            nc.scalar.copy(
                out=wide[:, HALF:NC16].rearrange("p c h (w r) -> p (c h w) r", r=2),
                in_=s1[:, HALF:NC16].rearrange("p c h w -> p (c h w)").unsqueeze(2).to_broadcast([P, HALF * 128, 2]),
            )

        w32 = wraw[:].bitcast(F32)
        wc, ws, wgrp = [], [], {}
        for br in range(2):
            wc.append(const.tile([P, G * 512], U32, name="wc%d" % br, align_bytes=64))
            ws.append(const.tile([P, G * 512], U8, name="ws%d" % br, align_bytes=64))

        def w_transposes(br):
            wgrp[br] = const.tile([P, G, 512, J], BF16, name="wgrp%d" % br, tag="wgrp", align_bytes=64)
            wg32 = wgrp[br][:].bitcast(F32)
            for g in range(G):
                for mp in range(2):
                    tp = psum.tile([P, 2, 2, P], F32, name="tp", tag="tp")
                    for u in range(2):
                        for mm in range(2):
                            nc.tensor.transpose(
                                tp[:, u, mm, :],
                                w32[:, br, 2 * mp + mm, 256 * g + u : 256 * (g + 1) : 2],
                                ident[:],
                            )
                    nc.scalar.copy(
                        out=wg32[:, g, 256 * mp : 256 * (mp + 1), :],
                        in_=tp[:].rearrange("p u m o -> p (m o) u"),
                    )

        def w_quant(br):
            nc.vector.quantize_mx(
                out=wc[br][:].bitcast(FP8X4),
                scales=ws[br][:],
                in_=wgrp[br][:].rearrange("p g o t -> p (g o t)"),
            )

        def quantise(src, codes, scales):
            nc.vector.quantize_mx(
                out=codes[:].rearrange("p g x -> p (g x)").bitcast(FP8X4),
                scales=scales[:].rearrange("p g x -> p (g x)"),
                in_=src[:].rearrange("p g x t -> p (g x t)"),
            )

        def passes(br, m, codes, scales):
            acc = psum.tile([P, 512], F32, name="acc", tag="acc", bufs=6)
            for g in range(G):
                cols = slice(512 * g + P * m, 512 * g + P * (m + 1))
                nc.tensor.matmul_mx(
                    out=acc[:],
                    lhsT=wc[br][:, cols].bitcast(FP8X4),
                    lhsT_scale=ws[br][:, cols],
                    rhs=codes[:, g, :].bitcast(FP8X4),
                    rhs_scale=scales[:, g, :],
                    start=(g == 0),
                    stop=(g == G - 1),
                )
            return acc

        f0v = f0[:].rearrange("p a (j h w) -> p a j h w", j=J, h=CH, w=CW)
        icod, isca, gi = [], [], {}
        for n in range(NS):
            icod.append(const.tile([P, G, 512], U32, name="icod%d" % n, align_bytes=64))
            isca.append(const.tile([P, G, 512], U8, name="isca%d" % n, align_bytes=64))

        def img_sum(n, g):
            if n not in gi:
                gi[n] = grp.tile([P, G, 512, J], BF16, name="gi%d" % n, tag="grp", align_bytes=64)
            a = n * G + g
            dst = gi[n][:, g].rearrange("p (h w) j -> p h w j", w=CW)
            fine = f0v[:, a].rearrange("p j h w -> p h w j")
            coarse = wide[:, a * J : (a + 1) * J].rearrange("p j h w -> p h w j")
            if n == 0:
                for r0, r1, a0, a1 in spans(8):
                    nc.vector.tensor_tensor(
                        out=dst[:, r0:r1],
                        in0=fine[:, r0:r1],
                        in1=coarse[:, a0:a1].to_broadcast([P, r1 - r0, CW, J]),
                        op=ALU.add,
                    )
            else:
                for r in range(2):
                    nc.vector.tensor_tensor(out=dst[:, r:CH:2], in0=fine[:, r:CH:2], in1=coarse, op=ALU.add)

        def img_quant(n):
            quantise(gi[n], icod[n], isca[n])

        out_view = out.rearrange("n (b p m) h w -> n b p m (h w)", b=2, p=P, m=MT)
        ist, iacc = {}, {}

        def img_mm(k):
            n, mp = divmod(k, 2)
            for mm in range(2):
                iacc[(k, mm)] = passes(0, 2 * mp + mm, icod[n], isca[n])

        def img_ev(k):
            n, mp = divmod(k, 2)
            ist[k] = big.tile([P, 2, 32, 64], F32, name="ist%d" % k, tag="big")
            for mm in range(2):
                bn_relu(ist[k][:, mm, 8:24, 16:48], iacc[(k, mm)][:].rearrange("p (h w) -> p h w", w=CW), 0, 2 * mp + mm)

        def img_xa(k):
            t = ist[k]
            nc.vector.tensor_copy(out=t[:, :, 8:24, 0:16], in_=t[:, :, 8:24, 16:17].to_broadcast([P, 2, 16, 16]))
            nc.vector.tensor_copy(out=t[:, :, 8:24, 48:64], in_=t[:, :, 8:24, 47:48].to_broadcast([P, 2, 16, 16]))

        def img_xb(k):
            n, mp = divmod(k, 2)
            t = ist[k]
            nc.vector.tensor_copy(out=t[:, :, 0:8, :], in_=t[:, :, 8:9, :].to_broadcast([P, 2, 8, 64]))
            nc.vector.tensor_copy(out=t[:, :, 24:32, :], in_=t[:, :, 23:24, :].to_broadcast([P, 2, 8, 64]))
            nc.sync.dma_start(out=out_view[n, 0, :, 2 * mp : 2 * mp + 2, :], in_=t[:].rearrange("p m h w -> p m (h w)"))

        gp, pcod, psca, pacc, pst = {}, {}, {}, {}, {}

        def regroup(n, g, q):
            i = n * NQ + q
            if i not in gp:
                gp[i] = grp.tile([P, G, 512, J], BF16, name="gp%d" % i, tag="grp", align_bytes=64)
            copy = nc.scalar.copy if (n, g, q) in SCALAR_UNITS else nc.vector.tensor_copy
            copy(
                out=gp[i][:, g].rearrange("p (c i) t -> p c t i", i=4),
                in_=raw[(n, g)][:, :, 512 * q : 512 * (q + 1)].rearrange("p t (c i) -> p c t i", i=4),
            )

        def pts_quant(i):
            pcod[i] = cod.tile([P, G, 512], U32, name="pcod", tag="pcod", align_bytes=64)
            psca[i] = cod.tile([P, G, 512], U8, name="psca", tag="psca", align_bytes=64)
            quantise(gp[i], pcod[i], psca[i])

        def pts_mm(i):
            for m in range(MT):
                pacc[(i, m)] = passes(1, m, pcod[i], psca[i])

        def pts_ev(i):
            n, q = divmod(i, NQ)
            if n in PAIRED:
                if q == 0:
                    for mp in range(2):
                        pst[(n, mp)] = big.tile([P, 2, HW], F32, name="pst%d%d" % (n, mp), tag="big")
                for m in range(MT):
                    bn_relu(pst[(n, m // 2)][:, m % 2, 512 * q : 512 * (q + 1)], pacc[(i, m)][:], 1, m)
                    if q == NQ - 1 and m % 2 == 1:
                        mp = m // 2
                        nc.sync.dma_start(out=out_view[n, 1, :, 2 * mp : 2 * mp + 2, :], in_=pst[(n, mp)][:])
                return
            half = q // 2
            cols = slice(1024 * half, 1024 * (half + 1))
            if q % 2 == 0:
                pst[(n, half)] = big.tile([P, MT, 1024], F32, name="pst%d%d" % (n, half), tag="big")
            t = pst[(n, half)]
            for m in range(MT):
                bn_relu(t[:, m, 512 * (q % 2) : 512 * (q % 2 + 1)], pacc[(i, m)][:], 1, m)
                if i == NS * NQ - 1:
                    nc.sync.dma_start(out=out_view[n, 1, :, m, cols], in_=t[:, m, :])
            if q % 2 == 1 and i != NS * NQ - 1:
                nc.sync.dma_start(out=out_view[n, 1, :, :, cols], in_=t[:])

        load_level(f4, img_feat4)
        load_level(f3, img_feat3)
        load_level(f2, img_feat2)
        load_level(f1, img_feat1)
        load_f0(0)
        load_w(0, img_w)
        load_f0(1)
        load_w(1, pts_w)
        load_raw(0, 0)
        load_raw(0, 1)
        load_raw(1, 0)
        load_raw(1, 1)
        load_bn(0, IMG_BN)
        load_bn(1, PTS_BN)
        level3()
        level2()
        level1()
        widen0()
        widen1()
        img_sum(0, 0)
        img_sum(0, 1)
        w_transposes(0)
        bn_turn(0)
        w_quant(0)
        bn_out(0)
        bn_sqrt(0)
        img_quant(0)
        bn_op(0, 0)
        bn_op(0, 1)
        bn_op(0, 2)
        img_sum(1, 0)
        bn_op(0, 3)
        bn_op(0, 4)
        w_transposes(1)
        bn_turn(1)
        img_mm(0)
        regroup(0, 0, 0)
        img_mm(1)
        img_sum(1, 1)
        img_ev(0)
        img_ev(1)
        img_xa(0)
        w_quant(1)
        img_xb(0)
        img_xa(1)
        img_quant(1)
        bn_out(1)
        regroup(0, 0, 1)
        img_xb(1)
        bn_sqrt(1)
        img_mm(2)
        img_mm(3)
        regroup(0, 1, 0)
        regroup(0, 0, 2)
        bn_op(1, 0)
        bn_op(1, 1)
        regroup(0, 1, 1)
        bn_op(1, 2)
        pts_quant(0)
        bn_op(1, 3)
        pts_quant(1)
        bn_op(1, 4)
        img_ev(2)
        regroup(0, 0, 3)
        img_ev(3)
        pts_mm(0)
        img_xa(2)
        regroup(0, 1, 2)
        img_xb(2)
        pts_ev(0)
        pts_mm(1)
        img_xa(3)
        pts_quant(2)
        regroup(0, 1, 3)
        img_xb(3)
        pts_ev(1)
        pts_quant(3)
        pts_mm(2)
        pts_ev(2)
        regroup(1, 0, 0)
        regroup(1, 1, 0)
        regroup(1, 0, 1)
        pts_mm(3)
        pts_quant(4)
        regroup(1, 1, 1)
        regroup(1, 0, 2)
        pts_quant(5)
        pts_ev(3)
        pts_mm(4)
        regroup(1, 1, 2)
        regroup(1, 0, 3)
        pts_ev(4)
        pts_mm(5)
        pts_quant(6)
        regroup(1, 1, 3)
        pts_ev(5)
        pts_mm(6)
        pts_quant(7)
        pts_ev(6)
        pts_mm(7)
        pts_ev(7)
